import numpy as np
import ml_dtypes


def mxq(x, axis, fmt="e4m3"):
    dtype, down = {"e4m3": (ml_dtypes.float8_e4m3fn, 7), "e5m2": (ml_dtypes.float8_e5m2, 14)}[fmt]
    v = np.moveaxis(np.asarray(x, np.float32).astype(ml_dtypes.bfloat16).astype(np.float64), axis, -1)
    blocks = v.reshape(v.shape[:-1] + (-1, 32))
    amax = np.abs(blocks).max(-1, keepdims=True)
    byte = np.maximum(np.where(amax > 0, np.frexp(amax)[1] - 1 + 127, 0) - down, 1)
    scale = np.exp2(byte - 127.0)
    codes = (blocks / scale).astype(np.float32).astype(dtype).astype(np.float64)
    return np.moveaxis((codes * scale).reshape(v.shape), -1, axis)


WIDE = False


def mx_kscale(k):
    if not WIDE:
        return np.ones(k)
    levels = np.array([10, -10, 5, -5, 0])
    if k % 512:
        return np.exp2(np.random.permutation(np.resize(levels, k // 32))).repeat(32)
    a = np.empty((k // 512, 16))
    for p in range(k // 512):
        a[p, :8] = np.random.permutation(np.resize(levels, 8))
        for g in range(8):
            far = levels[np.abs(levels - a[p, g]) >= 10]
            a[p, g + 8] = far[np.random.randint(len(far))]
    return np.exp2(a.ravel()).repeat(32)


BF16 = ml_dtypes.bfloat16


def bf(x):
    return np.asarray(x, np.float32).astype(BF16)


def f64(x):
    return np.asarray(x).astype(np.float64)


B, D, P, C, DEPTH = 512, 1024, 512, 128, 5
INT = (1 << DEPTH) - 1
TOT = INT + INT + 1
SIGMA = 1.0


def path_probs(th):
    prob = np.ones((1, th.shape[1]))
    probs = [prob]
    off = 0
    for d in range(DEPTH):
        n = 1 << d
        t = th[off:off + n]
        left = prob * (1.0 + t) * 0.5
        right = prob * (1.0 - t) * 0.5
        prob = np.stack([left, right], axis=1).reshape(n + n, -1)
        probs.append(prob)
        off += n
    return np.concatenate(probs, axis=0)


def setup_inputs():
    s, t = mx_kscale(D), mx_kscale(P)
    return {"X": bf(np.random.standard_normal((B, D)) * s),
            "Z": bf(np.random.standard_normal((P, D)) * 0.25 * P / np.sqrt(D) * t[:, None] / s),
            "W": bf(np.random.standard_normal((C * TOT, P)) * 4.0 / np.sqrt(P) / t),
            "V": bf(np.random.standard_normal((C * TOT, P)) * 4.0 / np.sqrt(P) / t),
            "th": bf(np.tanh(1.5 * np.random.standard_normal((INT, B))))}


def reference(X, Z, W, V, th):
    Xp = (mxq(f64(Z), 1, "e4m3") @ mxq(f64(X), 1, "e4m3").T) / P
    Xq = mxq(Xp, 0, "e4m3")
    WX = (mxq(f64(W), 1, "e4m3") @ Xq).reshape(TOT, C, B)
    VX = (mxq(f64(V), 1, "e4m3") @ Xq).reshape(TOT, C, B)
    probs = path_probs(f64(th))
    return np.sum(probs[:, None, :] * WX * np.tanh(SIGMA * VX), axis=0)

@@ -1,0 +1,316 @@
+from contextlib import ExitStack
+
+import concourse.mybir as mybir
+from concourse.masks import make_identity
+
+F32 = mybir.dt.float32
+BF16 = mybir.dt.bfloat16
+U32 = mybir.dt.uint32
+U8 = mybir.dt.uint8
+FP8X4 = mybir.dt.float8_e4m3fn_x4
+ADD = mybir.AluOpType.add
+MULT = mybir.AluOpType.mult
+TANH = mybir.ActivationFunctionType.Tanh
+
+P = 128
+PACK = 4
+K_PASS = P * PACK
+HALVES = 2
+
+SAMPLES, FEATURES, PROJECTED, CLASSES = 512, 1024, 512, 128
+DEPTH = 5
+INNER_NODES = (1 << DEPTH) - 1
+NODES = 2 * INNER_NODES + 1
+SAMPLE_TILES = SAMPLES // P
+FEATURE_PASSES = FEATURES // K_PASS
+GROUP_NODES = 4
+BANK_BLOCKS = 2
+
+STEP_TILES = 2
+STEPS = SAMPLE_TILES // STEP_TILES
+MATRICES = ("v", "w")
+RAW_BUFS = 6
+
+FLOPS = 2 * PROJECTED * SAMPLES * FEATURES + 2 * 2 * NODES * CLASSES * SAMPLES * PROJECTED
+
+
+def node_groups():
+    groups = []
+    first = 0
+    for size in (GROUP_NODES, 2, 1):
+        for repeat in range((NODES - first) // size):
+            groups.append((first, size))
+            first += size
+    return groups
+
+
+def tile_bonsailayer_pa_kernel(tc, X, Z, W, V, th, out):
+    nc = tc.nc
+    groups = node_groups()
+
+    with ExitStack() as ctx:
+        consts = ctx.enter_context(tc.tile_pool(name="consts", bufs=1))
+        first_stage = ctx.enter_context(tc.tile_pool(name="first_stage", bufs=4))
+        raw_pool = ctx.enter_context(tc.tile_pool(name="raw", bufs=RAW_BUFS))
+        grouped_pool = ctx.enter_context(tc.tile_pool(name="grouped", bufs=3))
+        codes_pool = ctx.enter_context(tc.tile_pool(name="codes", bufs=3))
+        work = ctx.enter_context(tc.tile_pool(name="work", bufs=4))
+        psum_words = ctx.enter_context(tc.psum_pool(name="psum_words", bufs=3))
+        psum_products = ctx.enter_context(tc.psum_pool(name="psum_products", bufs=2))
+        psum_score = ctx.enter_context(tc.psum_pool(name="psum_score", bufs=1))
+        ctx.enter_context(tc.manual_schedule())
+
+        ident_f32 = consts.tile([P, P], F32, name="ident_f32")
+        make_identity(nc, ident_f32[:])
+        ident_bf16 = consts.tile([P, P], BF16, name="ident_bf16")
+        make_identity(nc, ident_bf16[:])
+
+        th_rows = consts.tile([P, SAMPLES], BF16, name="th_rows")
+        nc.vector.memset(th_rows[:], 0.0)
+        nc.scalar.dma_start(out=th_rows[:INNER_NODES, :], in_=th)
+
+        warm = consts.tile([P, 1], F32, name="warm")
+        nc.vector.memset(warm[:], 0.0)
+        nc.scalar.activation(out=warm[:], in_=warm[:], func=TANH)
+
+        z_raw = consts.tile([P, PACK * FEATURES], BF16, name="z_raw")
+        for u in range(HALVES):
+            nc.sync.dma_start(
+                out=z_raw[:, u * 2 * FEATURES : (u + 1) * 2 * FEATURES],
+                in_=Z.rearrange("(q t) d -> q (t d)", t=PACK)[:, u * 2 * FEATURES : (u + 1) * 2 * FEATURES],
+            )
+        x_raw = consts.tile([P, SAMPLE_TILES * FEATURES], BF16, name="x_raw")
+        for s in range(SAMPLE_TILES):
+            nc.sync.dma_start(
+                out=x_raw[:, s * FEATURES : (s + 1) * FEATURES], in_=X[s * P : (s + 1) * P, :]
+            )
+
+        def transpose_blocks(words, blocks, grouped_words, copy):
+            bank = psum_words.tile([P, BANK_BLOCKS, HALVES, P], F32, name="bank", tag="bank")
+            for a in range(blocks):
+                for u in range(HALVES):
+                    first_word = a * HALVES * P
+                    nc.tensor.transpose(
+                        bank[:, a, u, :],
+                        words[:, first_word + u : first_word + HALVES * P : HALVES],
+                        ident_f32[:],
+                    )
+            copy(
+                out=grouped_words.rearrange("q (a r u) -> q a r u", a=blocks, u=HALVES),
+                in_=bank[:, :blocks].rearrange("q a u r -> q a r u"),
+            )
+
+        def quantise(grouped, codes, scales):
+            nc.vector.quantize_mx(out=codes.bitcast(FP8X4), scales=scales, in_=grouped)
+
+        def quantise_row_tiles(raw, name):
+            codes = consts.tile([P, PACK * FEATURE_PASSES * P], U32, name=name + "_codes", align_bytes=64)
+            scales = consts.tile([P, PACK * FEATURE_PASSES * P], U8, name=name + "_scales", align_bytes=64)
+            words = raw[:].bitcast(F32)
+            row_words = FEATURES // 2
+            grouped_tiles = []
+            for r in range(PACK):
+                grouped = first_stage.tile([P, FEATURES], BF16, name=name + "_grouped", tag="grouped", align_bytes=64)
+                copy = nc.scalar.copy if r % 2 == 0 else nc.vector.tensor_copy
+                transpose_blocks(
+                    words[:, r * row_words : (r + 1) * row_words],
+                    FEATURE_PASSES,
+                    grouped[:].bitcast(F32),
+                    copy,
+                )
+                grouped_tiles.append(grouped)
+            cols = FEATURE_PASSES * P
+            for r in range(PACK):
+                quantise(
+                    grouped_tiles[r][:],
+                    codes[:, r * cols : (r + 1) * cols],
+                    scales[:, r * cols : (r + 1) * cols],
+                )
+            return codes, scales
+
+        z_codes, z_scales = quantise_row_tiles(z_raw, "z")
+        x_codes, x_scales = quantise_row_tiles(x_raw, "x")
+
+        raw_tiles = {}
+
+        def load_matrix(g, name):
+            first_node, count = groups[g]
+            matrix = V if name == "v" else W
+            raw = raw_pool.tile([P, GROUP_NODES * PROJECTED], BF16, name="raw_" + name, tag="raw_" + name)
+            nc.sync.dma_start(
+                out=raw[:, : count * PROJECTED].rearrange("c (j k) -> c j k", j=count),
+                in_=matrix[first_node * P : (first_node + count) * P, :].rearrange("(j c) k -> c j k", c=P),
+            )
+            raw_tiles[(g, name)] = raw
+
+        for g in range(RAW_BUFS):
+            for name in MATRICES:
+                load_matrix(g, name)
+
+        th_cols = psum_words.tile([P, SAMPLE_TILES, P], BF16, name="th_cols", tag="bank")
+        for s in range(SAMPLE_TILES):
+            nc.tensor.transpose(th_cols[:, s, :], th_rows[:, s * P : (s + 1) * P], ident_bf16[:])
+        branch = consts.tile([P, SAMPLE_TILES, INNER_NODES, 2], F32, name="branch")
+        for side, sign in ((0, 0.5), (1, -0.5)):
+            nc.vector.tensor_scalar(
+                out=branch[:, :, :, side],
+                in0=th_cols[:, :, :INNER_NODES],
+                scalar1=sign,
+                scalar2=0.5,
+                op0=MULT,
+                op1=ADD,
+            )
+        prob = consts.tile([P, SAMPLE_TILES, NODES], F32, name="prob")
+        nc.vector.memset(prob[:, :, 0:1], 1.0)
+        first = 0
+        for depth in range(DEPTH):
+            width = 1 << depth
+            child = 2 * first + 1
+            nc.vector.tensor_tensor(
+                out=prob[:, :, child : child + 2 * width].rearrange("b s (i c) -> b s i c", c=2),
+                in0=branch[:, :, first : first + width, :],
+                in1=prob[:, :, first : first + width]
+                .unsqueeze(3)
+                .to_broadcast([P, SAMPLE_TILES, width, 2]),
+                op=MULT,
+            )
+            first = child
+
+        xq_codes = consts.tile([P, SAMPLES], U32, name="xq_codes", align_bytes=64)
+        xq_scales = consts.tile([P, SAMPLES], U8, name="xq_scales", align_bytes=64)
+        for s in range(SAMPLE_TILES):
+            xp = psum_products.tile([P, PACK, P], F32, name="xp", tag="wx")
+            for t in range(PACK):
+                for g in range(FEATURE_PASSES):
+                    z_cols = slice((t * FEATURE_PASSES + g) * P, (t * FEATURE_PASSES + g + 1) * P)
+                    x_cols = slice((s * FEATURE_PASSES + g) * P, (s * FEATURE_PASSES + g + 1) * P)
+                    nc.tensor.matmul_mx(
+                        out=xp[:, t, :],
+                        lhsT=z_codes[:, z_cols].bitcast(FP8X4),
+                        lhsT_scale=z_scales[:, z_cols],
+                        rhs=x_codes[:, x_cols].bitcast(FP8X4),
+                        rhs_scale=x_scales[:, x_cols],
+                        start=(g == 0),
+                        stop=(g == FEATURE_PASSES - 1),
+                    )
+            xp_grouped = first_stage.tile([P, P * PACK], BF16, name="xp_grouped", tag="xp_grouped", align_bytes=64)
+            nc.scalar.mul(
+                out=xp_grouped[:].rearrange("q (b t) -> q b t", t=PACK),
+                in_=xp[:].rearrange("q t b -> q b t"),
+                mul=1.0 / PROJECTED,
+            )
+            quantise(xp_grouped[:], xq_codes[:, s * P : (s + 1) * P], xq_scales[:, s * P : (s + 1) * P])
+
+        grouped_tiles = {}
+        code_tiles = {}
+        score = psum_score.tile([P, SAMPLES], F32, name="score")
+        sums = [consts.tile([P, GROUP_NODES * CLASSES], F32, name="sum_%d" % h) for h in range(STEPS)]
+
+        def transpose_matrix(g, name):
+            count = groups[g][1]
+            block_words = PROJECTED // 2
+            words = raw_tiles[(g, name)][:].bitcast(F32)
+            grouped = grouped_pool.tile([P, GROUP_NODES * PROJECTED], BF16, name="grouped_" + name, tag="grouped_" + name, align_bytes=64)
+            grouped_words = grouped[:].bitcast(F32)
+            for j in range(0, count, BANK_BLOCKS):
+                blocks = min(BANK_BLOCKS, count - j)
+                part = slice(j * block_words, (j + blocks) * block_words)
+                transpose_blocks(words[:, part], blocks, grouped_words[:, part], nc.scalar.copy)
+            grouped_tiles[(g, name)] = grouped
+            if g + RAW_BUFS < len(groups):
+                load_matrix(g + RAW_BUFS, name)
+
+        def quantise_matrix(g, name):
+            count = groups[g][1]
+            codes = codes_pool.tile([P, GROUP_NODES * CLASSES], U32, name="codes_" + name, tag="codes_" + name, align_bytes=64)
+            scales = codes_pool.tile([P, GROUP_NODES * CLASSES], U8, name="scales_" + name, tag="scales_" + name, align_bytes=64)
+            quantise(
+                grouped_tiles[(g, name)][:, : count * PROJECTED],
+                codes[:, : count * CLASSES],
+                scales[:, : count * CLASSES],
+            )
+            code_tiles[(g, name)] = (codes, scales)
+
+        def add_to_score(s, products, count, opens=False, closes=False):
+            for j in range(count):
+                nc.tensor.matmul(
+                    out=score[:, s * P : (s + 1) * P],
+                    lhsT=products[:, j * CLASSES : (j + 1) * CLASSES],
+                    rhs=ident_f32[:],
+                    is_transpose=True,
+                    start=(opens and j == 0),
+                    stop=(closes and j == count - 1),
+                )
+
+        def multiply_step(g, h):
+            first_node, count = groups[g]
+            cols = count * CLASSES
+            tiles = range(h * STEP_TILES, (h + 1) * STEP_TILES)
+            accs = {}
+            for name in MATRICES:
+                codes, scales = code_tiles[(g, name)]
+                for s in tiles:
+                    acc = psum_products.tile([P, GROUP_NODES * CLASSES], F32, name=name + "x", tag=name + "x")
+                    nc.tensor.matmul_mx(
+                        out=acc[:, :cols],
+                        lhsT=xq_codes[:, s * P : (s + 1) * P].bitcast(FP8X4),
+                        lhsT_scale=xq_scales[:, s * P : (s + 1) * P],
+                        rhs=codes[:, :cols].bitcast(FP8X4),
+                        rhs_scale=scales[:, :cols],
+                        start=True,
+                        stop=True,
+                    )
+                    accs[(name, s)] = acc
+            step_products = []
+            for s in tiles:
+                tanh_vx = work.tile([P, GROUP_NODES * CLASSES], F32, name="tanh_vx", tag="tanh_vx")
+                nc.scalar.activation(out=tanh_vx[:, :cols], in_=accs[("v", s)][:, :cols], func=TANH)
+                if g == 0 and s % 2 == 1:
+                    products = sums[h]
+                else:
+                    products = work.tile([P, GROUP_NODES * CLASSES], F32, name="products", tag="products", bufs=6)
+                for j in range(count):
+                    node_cols = slice(j * CLASSES, (j + 1) * CLASSES)
+                    nc.vector.scalar_tensor_tensor(
+                        out=products[:, node_cols],
+                        in0=accs[("w", s)][:, node_cols],
+                        scalar=prob[:, s, first_node + j : first_node + j + 1],
+                        in1=tanh_vx[:, node_cols],
+                        op0=MULT,
+                        op1=MULT,
+                    )
+                step_products.append(products)
+            return step_products
+
+        def add_step(g, h, step_products):
+            count = groups[g][1]
+            cols = count * CLASSES
+            add_to_score(h * STEP_TILES, step_products[0], count, opens=(g == 0 and h == 0))
+            if g > 0:
+                nc.gpsimd.tensor_tensor(
+                    out=sums[h][:, :cols], in0=sums[h][:, :cols], in1=step_products[1][:, :cols], op=ADD
+                )
+
+        for g in range(2):
+            for name in MATRICES:
+                transpose_matrix(g, name)
+        for name in MATRICES:
+            quantise_matrix(0, name)
+        earlier = None
+        for g in range(len(groups)):
+            for h in range(STEPS):
+                if g + 1 < len(groups):
+                    quantise_matrix(g + 1, MATRICES[h])
+                step_products = multiply_step(g, h)
+                if g + 2 < len(groups):
+                    transpose_matrix(g + 2, MATRICES[h])
+                if earlier is not None:
+                    add_step(*earlier)
+                earlier = (g, h, step_products)
+        add_step(*earlier)
+        for h in range(STEPS):
+            add_to_score(h * STEP_TILES + 1, sums[h], GROUP_NODES, closes=(h == STEPS - 1))
+
+        result = consts.tile([P, SAMPLES], F32, name="result")
+        nc.scalar.copy(out=result[:], in_=score[:])
+        nc.sync.dma_start(out=out, in_=result[:])

@@ -29,7 +29,26 @@ BANK_BLOCKS = 2
 STEP_TILES = 2
 STEPS = SAMPLE_TILES // STEP_TILES
 MATRICES = ("v", "w")
-RAW_BUFS = 6
+LOADED_AHEAD = 6
+RAW_BUFS = 8
+ADD_PARTS = 2
+VEC_TILES = ()
+Q_AT = 0
+VVWW = True
+SUMS_FIRST = False
+
+
+BUFS = {"words": 3, "v": 2, "w": 2}
+MX_ORDER = (("v", 0), ("w", 0), ("v", 1), ("w", 1), ("v", 2), ("w", 2), ("v", 3), ("w", 3))
+QW_AFTER = 1
+RE_AFTER = 2
+REORDER = ()
+SS, SV, VS = (0, 0), (0, 1), (1, 0)
+COPIES_VI = SS
+COPIES_WI = SS
+PRODUCT_BUFS = 8
+POOL_TILES = (0, 2)
+DIRECT_FROM = 16
 
 FLOPS = 2 * PROJECTED * SAMPLES * FEATURES + 2 * 2 * NODES * CLASSES * SAMPLES * PROJECTED
 
@@ -55,7 +74,7 @@ def tile_bonsailayer_pa_kernel(tc, X, Z, W, V, th, out):
         grouped_pool = ctx.enter_context(tc.tile_pool(name="grouped", bufs=3))
         codes_pool = ctx.enter_context(tc.tile_pool(name="codes", bufs=3))
         work = ctx.enter_context(tc.tile_pool(name="work", bufs=4))
-        psum_words = ctx.enter_context(tc.psum_pool(name="psum_words", bufs=3))
+        psum_words = ctx.enter_context(tc.psum_pool(name="psum_words", bufs=BUFS["words"]))
         psum_products = ctx.enter_context(tc.psum_pool(name="psum_products", bufs=2))
         psum_score = ctx.enter_context(tc.psum_pool(name="psum_score", bufs=1))
         ctx.enter_context(tc.manual_schedule())
@@ -74,64 +93,15 @@ def tile_bonsailayer_pa_kernel(tc, X, Z, W, V, th, out):
         nc.scalar.activation(out=warm[:], in_=warm[:], func=TANH)
 
         z_raw = consts.tile([P, PACK * FEATURES], BF16, name="z_raw")
-        for u in range(HALVES):
-            nc.sync.dma_start(
-                out=z_raw[:, u * 2 * FEATURES : (u + 1) * 2 * FEATURES],
-                in_=Z.rearrange("(q t) d -> q (t d)", t=PACK)[:, u * 2 * FEATURES : (u + 1) * 2 * FEATURES],
-            )
         x_raw = consts.tile([P, SAMPLE_TILES * FEATURES], BF16, name="x_raw")
-        for s in range(SAMPLE_TILES):
-            nc.sync.dma_start(
-                out=x_raw[:, s * FEATURES : (s + 1) * FEATURES], in_=X[s * P : (s + 1) * P, :]
-            )
-
-        def transpose_blocks(words, blocks, grouped_words, copy):
-            bank = psum_words.tile([P, BANK_BLOCKS, HALVES, P], F32, name="bank", tag="bank")
-            for a in range(blocks):
-                for u in range(HALVES):
-                    first_word = a * HALVES * P
-                    nc.tensor.transpose(
-                        bank[:, a, u, :],
-                        words[:, first_word + u : first_word + HALVES * P : HALVES],
-                        ident_f32[:],
-                    )
-            copy(
-                out=grouped_words.rearrange("q (a r u) -> q a r u", a=blocks, u=HALVES),
-                in_=bank[:, :blocks].rearrange("q a u r -> q a r u"),
-            )
-
-        def quantise(grouped, codes, scales):
-            nc.vector.quantize_mx(out=codes.bitcast(FP8X4), scales=scales, in_=grouped)
-
-        def quantise_row_tiles(raw, name):
-            codes = consts.tile([P, PACK * FEATURE_PASSES * P], U32, name=name + "_codes", align_bytes=64)
-            scales = consts.tile([P, PACK * FEATURE_PASSES * P], U8, name=name + "_scales", align_bytes=64)
-            words = raw[:].bitcast(F32)
-            row_words = FEATURES // 2
-            grouped_tiles = []
-            for r in range(PACK):
-                grouped = first_stage.tile([P, FEATURES], BF16, name=name + "_grouped", tag="grouped", align_bytes=64)
-                copy = nc.scalar.copy if r % 2 == 0 else nc.vector.tensor_copy
-                transpose_blocks(
-                    words[:, r * row_words : (r + 1) * row_words],
-                    FEATURE_PASSES,
-                    grouped[:].bitcast(F32),
-                    copy,
-                )
-                grouped_tiles.append(grouped)
-            cols = FEATURE_PASSES * P
-            for r in range(PACK):
-                quantise(
-                    grouped_tiles[r][:],
-                    codes[:, r * cols : (r + 1) * cols],
-                    scales[:, r * cols : (r + 1) * cols],
-                )
-            return codes, scales
-
-        z_codes, z_scales = quantise_row_tiles(z_raw, "z")
-        x_codes, x_scales = quantise_row_tiles(x_raw, "x")
-
         raw_tiles = {}
+
+        def load_z(t):
+            cols = slice(t * FEATURES, (t + 1) * FEATURES)
+            nc.sync.dma_start(out=z_raw[:, cols], in_=Z.rearrange("(q t) d -> q (t d)", t=PACK)[:, cols])
+
+        def load_x(s):
+            nc.sync.dma_start(out=x_raw[:, s * FEATURES : (s + 1) * FEATURES], in_=X[s * P : (s + 1) * P, :])
 
         def load_matrix(g, name):
             first_node, count = groups[g]
@@ -143,43 +113,65 @@ def tile_bonsailayer_pa_kernel(tc, X, Z, W, V, th, out):
             )
             raw_tiles[(g, name)] = raw
 
-        for g in range(RAW_BUFS):
+        for t in range(PACK):
+            load_z(t)
+        load_x(0)
+        load_x(1)
+        load_matrix(0, "v")
+        load_matrix(0, "w")
+        load_x(2)
+        load_x(3)
+        for g in range(1, LOADED_AHEAD):
             for name in MATRICES:
                 load_matrix(g, name)
 
-        th_cols = psum_words.tile([P, SAMPLE_TILES, P], BF16, name="th_cols", tag="bank")
-        for s in range(SAMPLE_TILES):
-            nc.tensor.transpose(th_cols[:, s, :], th_rows[:, s * P : (s + 1) * P], ident_bf16[:])
-        branch = consts.tile([P, SAMPLE_TILES, INNER_NODES, 2], F32, name="branch")
-        for side, sign in ((0, 0.5), (1, -0.5)):
-            nc.vector.tensor_scalar(
-                out=branch[:, :, :, side],
-                in0=th_cols[:, :, :INNER_NODES],
-                scalar1=sign,
-                scalar2=0.5,
-                op0=MULT,
-                op1=ADD,
+        def transpose_blocks(words, blocks, grouped_words, copy):
+            bank = psum_words.tile([P, BANK_BLOCKS, HALVES, P], F32, name="bank", tag="bank")
+            for a in range(blocks):
+                for u in range(HALVES):
+                    first_word = a * HALVES * P
+                    part = words[:, first_word + u : first_word + HALVES * P : HALVES]
+                    nc.tensor.transpose(bank[:, a, u, :], part, ident_f32[:])
+            copy(
+                out=grouped_words.rearrange("q (a r u) -> q a r u", a=blocks, u=HALVES),
+                in_=bank[:, :blocks].rearrange("q a u r -> q a r u"),
             )
-        prob = consts.tile([P, SAMPLE_TILES, NODES], F32, name="prob")
-        nc.vector.memset(prob[:, :, 0:1], 1.0)
-        first = 0
-        for depth in range(DEPTH):
-            width = 1 << depth
-            child = 2 * first + 1
-            nc.vector.tensor_tensor(
-                out=prob[:, :, child : child + 2 * width].rearrange("b s (i c) -> b s i c", c=2),
-                in0=branch[:, :, first : first + width, :],
-                in1=prob[:, :, first : first + width]
-                .unsqueeze(3)
-                .to_broadcast([P, SAMPLE_TILES, width, 2]),
-                op=MULT,
+
+        def quantise(grouped, codes, scales):
+            nc.vector.quantize_mx(out=codes.bitcast(FP8X4), scales=scales, in_=grouped)
+
+        z_codes = consts.tile([P, PACK * FEATURE_PASSES * P], U32, name="z_codes", align_bytes=64)
+        z_scales = consts.tile([P, PACK * FEATURE_PASSES * P], U8, name="z_scales", align_bytes=64)
+        x_codes = consts.tile([P, SAMPLE_TILES * FEATURE_PASSES * P], U32, name="x_codes", align_bytes=64)
+        x_scales = consts.tile([P, SAMPLE_TILES * FEATURE_PASSES * P], U8, name="x_scales", align_bytes=64)
+        first_stage_operands = {"z": (z_raw, z_codes, z_scales), "x": (x_raw, x_codes, x_scales)}
+        first_stage_grouped = {}
+
+        def transpose_row_tile(name, r, copy):
+            raw = first_stage_operands[name][0]
+            words = raw[:].bitcast(F32)
+            row_words = FEATURES // 2
+            grouped = first_stage.tile([P, FEATURES], BF16, name="row_grouped", tag="row_grouped", align_bytes=64)
+            transpose_blocks(
+                words[:, r * row_words : (r + 1) * row_words], FEATURE_PASSES, grouped[:].bitcast(F32), copy
             )
-            first = child
+            first_stage_grouped[(name, r)] = grouped
+
+        def quantise_row_tile(name, r):
+            codes, scales = first_stage_operands[name][1:]
+            cols = FEATURE_PASSES * P
+            quantise(
+                first_stage_grouped[(name, r)][:],
+                codes[:, r * cols : (r + 1) * cols],
+                scales[:, r * cols : (r + 1) * cols],
+            )
 
         xq_codes = consts.tile([P, SAMPLES], U32, name="xq_codes", align_bytes=64)
         xq_scales = consts.tile([P, SAMPLES], U8, name="xq_scales", align_bytes=64)
-        for s in range(SAMPLE_TILES):
-            xp = psum_products.tile([P, PACK, P], F32, name="xp", tag="wx")
+        xp_grouped_tiles = {}
+
+        def project(s):
+            xp = psum_products.tile([P, PACK, P], F32, name="xp", tag="wx", bufs=BUFS["w"])
             for t in range(PACK):
                 for g in range(FEATURE_PASSES):
                     z_cols = slice((t * FEATURE_PASSES + g) * P, (t * FEATURE_PASSES + g + 1) * P)
@@ -199,14 +191,48 @@ def tile_bonsailayer_pa_kernel(tc, X, Z, W, V, th, out):
                 in_=xp[:].rearrange("q t b -> q b t"),
                 mul=1.0 / PROJECTED,
             )
-            quantise(xp_grouped[:], xq_codes[:, s * P : (s + 1) * P], xq_scales[:, s * P : (s + 1) * P])
+            xp_grouped_tiles[s] = xp_grouped
+
+        def quantise_projection(s):
+            quantise(xp_grouped_tiles[s][:], xq_codes[:, s * P : (s + 1) * P], xq_scales[:, s * P : (s + 1) * P])
+
+        prob = consts.tile([P, SAMPLE_TILES, NODES], F32, name="prob")
+
+        def path_probabilities():
+            th_cols = psum_words.tile([P, SAMPLE_TILES, P], BF16, name="th_cols", tag="bank")
+            for s in range(SAMPLE_TILES):
+                nc.tensor.transpose(th_cols[:, s, :], th_rows[:, s * P : (s + 1) * P], ident_bf16[:])
+            branch = consts.tile([P, SAMPLE_TILES, INNER_NODES, 2], F32, name="branch")
+            for side, sign in ((0, 0.5), (1, -0.5)):
+                nc.vector.tensor_scalar(
+                    out=branch[:, :, :, side],
+                    in0=th_cols[:, :, :INNER_NODES],
+                    scalar1=sign,
+                    scalar2=0.5,
+                    op0=MULT,
+                    op1=ADD,
+                )
+            nc.gpsimd.memset(prob[:, :, 0:1], 1.0)
+            first = 0
+            for depth in range(DEPTH):
+                width = 1 << depth
+                child = 2 * first + 1
+                nc.gpsimd.tensor_tensor(
+                    out=prob[:, :, child : child + 2 * width].rearrange("b s (i c) -> b s i c", c=2),
+                    in0=branch[:, :, first : first + width, :],
+                    in1=prob[:, :, first : first + width]
+                    .unsqueeze(3)
+                    .to_broadcast([P, SAMPLE_TILES, width, 2]),
+                    op=MULT,
+                )
+                first = child
 
         grouped_tiles = {}
         code_tiles = {}
         score = psum_score.tile([P, SAMPLES], F32, name="score")
-        sums = [consts.tile([P, GROUP_NODES * CLASSES], F32, name="sum_%d" % h) for h in range(STEPS)]
+        sums = {s: consts.tile([P, GROUP_NODES * CLASSES], F32, name="sum_%d" % s) for s in POOL_TILES + VEC_TILES}
 
-        def transpose_matrix(g, name):
+        def transpose_matrix(g, name, copies):
             count = groups[g][1]
             block_words = PROJECTED // 2
             words = raw_tiles[(g, name)][:].bitcast(F32)
@@ -215,10 +241,8 @@ def tile_bonsailayer_pa_kernel(tc, X, Z, W, V, th, out):
             for j in range(0, count, BANK_BLOCKS):
                 blocks = min(BANK_BLOCKS, count - j)
                 part = slice(j * block_words, (j + blocks) * block_words)
-                transpose_blocks(words[:, part], blocks, grouped_words[:, part], nc.scalar.copy)
+                transpose_blocks(words[:, part], blocks, grouped_words[:, part], copies[j // BANK_BLOCKS])
             grouped_tiles[(g, name)] = grouped
-            if g + RAW_BUFS < len(groups):
-                load_matrix(g + RAW_BUFS, name)
 
         def quantise_matrix(g, name):
             count = groups[g][1]
@@ -242,74 +266,127 @@ def tile_bonsailayer_pa_kernel(tc, X, Z, W, V, th, out):
                     stop=(closes and j == count - 1),
                 )
 
-        def multiply_step(g, h):
+        def multiply(g, name, s, accs):
+            cols = groups[g][1] * CLASSES
+            codes, scales = code_tiles[(g, name)]
+            acc = psum_products.tile([P, GROUP_NODES * CLASSES], F32, name=name + "x", tag=name + "x", bufs=BUFS[name])
+            nc.tensor.matmul_mx(
+                out=acc[:, :cols],
+                lhsT=xq_codes[:, s * P : (s + 1) * P].bitcast(FP8X4),
+                lhsT_scale=xq_scales[:, s * P : (s + 1) * P],
+                rhs=codes[:, :cols].bitcast(FP8X4),
+                rhs_scale=scales[:, :cols],
+                start=True,
+                stop=True,
+            )
+            accs[(name, s)] = acc
+
+        def combine(g, s, accs):
             first_node, count = groups[g]
             cols = count * CLASSES
-            tiles = range(h * STEP_TILES, (h + 1) * STEP_TILES)
-            accs = {}
-            for name in MATRICES:
-                codes, scales = code_tiles[(g, name)]
-                for s in tiles:
-                    acc = psum_products.tile([P, GROUP_NODES * CLASSES], F32, name=name + "x", tag=name + "x")
-                    nc.tensor.matmul_mx(
-                        out=acc[:, :cols],
-                        lhsT=xq_codes[:, s * P : (s + 1) * P].bitcast(FP8X4),
-                        lhsT_scale=xq_scales[:, s * P : (s + 1) * P],
-                        rhs=codes[:, :cols].bitcast(FP8X4),
-                        rhs_scale=scales[:, :cols],
-                        start=True,
-                        stop=True,
-                    )
-                    accs[(name, s)] = acc
-            step_products = []
-            for s in tiles:
-                tanh_vx = work.tile([P, GROUP_NODES * CLASSES], F32, name="tanh_vx", tag="tanh_vx")
-                nc.scalar.activation(out=tanh_vx[:, :cols], in_=accs[("v", s)][:, :cols], func=TANH)
-                if g == 0 and s % 2 == 1:
-                    products = sums[h]
-                else:
-                    products = work.tile([P, GROUP_NODES * CLASSES], F32, name="products", tag="products", bufs=6)
-                for j in range(count):
-                    node_cols = slice(j * CLASSES, (j + 1) * CLASSES)
-                    nc.vector.scalar_tensor_tensor(
-                        out=products[:, node_cols],
-                        in0=accs[("w", s)][:, node_cols],
-                        scalar=prob[:, s, first_node + j : first_node + j + 1],
-                        in1=tanh_vx[:, node_cols],
-                        op0=MULT,
-                        op1=MULT,
-                    )
-                step_products.append(products)
-            return step_products
+            tanh_vx = work.tile([P, GROUP_NODES * CLASSES], F32, name="tanh_vx", tag="tanh_vx")
+            nc.scalar.activation(out=tanh_vx[:, :cols], in_=accs[("v", s)][:, :cols], func=TANH)
+            if g == 0 and s in POOL_TILES + VEC_TILES:
+                products = sums[s]
+            else:
+                products = work.tile([P, GROUP_NODES * CLASSES], F32, name="products", tag="products", bufs=PRODUCT_BUFS)
+            for j in range(count):
+                node_cols = slice(j * CLASSES, (j + 1) * CLASSES)
+                nc.vector.scalar_tensor_tensor(
+                    out=products[:, node_cols],
+                    in0=accs[("w", s)][:, node_cols],
+                    scalar=prob[:, s, first_node + j : first_node + j + 1],
+                    in1=tanh_vx[:, node_cols],
+                    op0=MULT,
+                    op1=MULT,
+                )
+            return products
 
-        def add_step(g, h, step_products):
+        score_opened = []
+
+        def add_step(g, step_products):
             count = groups[g][1]
             cols = count * CLASSES
-            add_to_score(h * STEP_TILES, step_products[0], count, opens=(g == 0 and h == 0))
-            if g > 0:
-                nc.gpsimd.tensor_tensor(
-                    out=sums[h][:, :cols], in0=sums[h][:, :cols], in1=step_products[1][:, :cols], op=ADD
-                )
+            for s, products in step_products:
+                if s in POOL_TILES + VEC_TILES and g < DIRECT_FROM:
+                    if g > 0:
+                        engine = nc.gpsimd if s in POOL_TILES else nc.vector
+                        part = cols // ADD_PARTS if s in POOL_TILES else cols
+                        for c in range(0, cols, part):
+                            cs = slice(c, c + part)
+                            engine.tensor_tensor(out=sums[s][:, cs], in0=sums[s][:, cs], in1=products[:, cs], op=ADD)
+                else:
+                    last = g == len(groups) - 1 and s == SAMPLE_TILES - 1
+                    add_to_score(s, products, count, opens=not score_opened, closes=last)
+                    score_opened.append(s)
 
-        for g in range(2):
-            for name in MATRICES:
-                transpose_matrix(g, name)
-        for name in MATRICES:
-            quantise_matrix(0, name)
+        by_scalar, by_vector = nc.scalar.copy, nc.vector.tensor_copy
+        COPIES_V = [(by_scalar, by_vector)[i] for i in COPIES_VI]
+        COPIES_W = [(by_scalar, by_vector)[i] for i in COPIES_WI]
+        transpose_row_tile("z", 0, by_scalar)
+        transpose_row_tile("z", 1, by_vector)
+        transpose_row_tile("z", 2, by_scalar)
+        quantise_row_tile("z", 0)
+        transpose_row_tile("z", 3, by_scalar)
+        quantise_row_tile("z", 1)
+        transpose_row_tile("x", 0, by_vector)
+        quantise_row_tile("z", 2)
+        transpose_row_tile("x", 1, by_scalar)
+        quantise_row_tile("z", 3)
+        quantise_row_tile("x", 0)
+        path_probabilities()
+        quantise_row_tile("x", 1)
+        transpose_matrix(0, "v", (by_scalar, by_vector))
+        project(0)
+        project(1)
+        quantise_matrix(0, "v")
+        transpose_matrix(0, "w", (by_scalar, by_vector))
+        quantise_projection(0)
+        quantise_projection(1)
+        transpose_row_tile("x", 2, by_scalar)
+        quantise_matrix(0, "w")
+        transpose_row_tile("x", 3, by_scalar)
+        transpose_matrix(1, "v", (by_vector, by_scalar))
+        quantise_row_tile("x", 2)
+        quantise_row_tile("x", 3)
+
         earlier = None
-        for g in range(len(groups)):
+        n_groups = len(groups)
+        for g in range(n_groups):
             for h in range(STEPS):
-                if g + 1 < len(groups):
-                    quantise_matrix(g + 1, MATRICES[h])
-                step_products = multiply_step(g, h)
-                if g + 2 < len(groups):
-                    transpose_matrix(g + 2, MATRICES[h])
-                if earlier is not None:
+                name = MATRICES[h]
+                if g == 0 and h == 1:
+                    project(2)
+                    project(3)
+                    transpose_matrix(1, "w", (by_scalar, by_vector))
+                    quantise_projection(2)
+                    quantise_projection(3)
+                accs = {}
+                s0, s1 = 2 * h, 2 * h + 1
+                if Q_AT == 0 and g + 1 < n_groups:
+                    quantise_matrix(g + 1, name)
+                for m, s in (("v", s0), ("v", s1), ("w", s0), ("w", s1)) if VVWW else (("v", s0), ("w", s0), ("v", s1), ("w", s1)):
+                    multiply(g, m, s, accs)
+                products = [(s0, combine(g, s0, accs))]
+                if Q_AT == 1 and g + 1 < n_groups:
+                    quantise_matrix(g + 1, name)
+                products.append((s1, combine(g, s1, accs)))
+                if Q_AT == 2 and g + 1 < n_groups:
+                    quantise_matrix(g + 1, name)
+                if SUMS_FIRST and earlier is not None:
                     add_step(*earlier)
-                earlier = (g, h, step_products)
+                if g + 2 < n_groups:
+                    transpose_matrix(g + 2, name, COPIES_V if h == 0 else COPIES_W)
+                if not SUMS_FIRST and earlier is not None:
+                    add_step(*earlier)
+                if g == DIRECT_FROM and h == 0:
+                    for s in POOL_TILES + VEC_TILES:
+                        add_to_score(s, sums[s], GROUP_NODES, opens=not score_opened)
+                        score_opened.append(s)
+                if g + LOADED_AHEAD < n_groups:
+                    load_matrix(g + LOADED_AHEAD, name)
+                earlier = (g, products)
         add_step(*earlier)
-        for h in range(STEPS):
-            add_to_score(h * STEP_TILES + 1, sums[h], GROUP_NODES, closes=(h == STEPS - 1))
 
         result = consts.tile([P, SAMPLES], F32, name="result")
         nc.scalar.copy(out=result[:], in_=score[:])

@@ -32,10 +32,11 @@ MATRICES = ("v", "w")
 LOADED_AHEAD = 6
 RAW_BUFS = 8
 ADD_PARTS = 2
-VEC_TILES = ()
+VEC_TILES = (0, 2)
 Q_AT = 0
 VVWW = True
 SUMS_FIRST = False
+SUMS_AT = 1
 
 
 BUFS = {"words": 3, "v": 2, "w": 2}
@@ -47,20 +48,24 @@ SS, SV, VS = (0, 0), (0, 1), (1, 0)
 COPIES_VI = SS
 COPIES_WI = SS
 PRODUCT_BUFS = 8
-POOL_TILES = (0, 2)
-DIRECT_FROM = 16
+POOL_TILES = ()
+DIRECT_FROM = 15
 
 FLOPS = 2 * PROJECTED * SAMPLES * FEATURES + 2 * 2 * NODES * CLASSES * SAMPLES * PROJECTED
 
 
 def node_groups():
-    groups = []
+    return [(first, min(GROUP_NODES, NODES - first)) for first in range(0, NODES, GROUP_NODES)]
+
+
+def node_runs(count):
+    runs = []
     first = 0
-    for size in (GROUP_NODES, 2, 1):
-        for repeat in range((NODES - first) // size):
-            groups.append((first, size))
+    for size in (4, 2, 1):
+        while count - first >= size:
+            runs.append((first, size))
             first += size
-    return groups
+    return runs
 
 
 def tile_bonsailayer_pa_kernel(tc, X, Z, W, V, th, out):
@@ -248,11 +253,13 @@ def tile_bonsailayer_pa_kernel(tc, X, Z, W, V, th, out):
             count = groups[g][1]
             codes = codes_pool.tile([P, GROUP_NODES * CLASSES], U32, name="codes_" + name, tag="codes_" + name, align_bytes=64)
             scales = codes_pool.tile([P, GROUP_NODES * CLASSES], U8, name="scales_" + name, tag="scales_" + name, align_bytes=64)
-            quantise(
-                grouped_tiles[(g, name)][:, : count * PROJECTED],
-                codes[:, : count * CLASSES],
-                scales[:, : count * CLASSES],
-            )
+            for first, size in node_runs(count):
+                cols = slice(first * CLASSES, (first + size) * CLASSES)
+                quantise(
+                    grouped_tiles[(g, name)][:, first * PROJECTED : (first + size) * PROJECTED],
+                    codes[:, cols],
+                    scales[:, cols],
+                )
             code_tiles[(g, name)] = (codes, scales)
 
         def add_to_score(s, products, count, opens=False, closes=False):
@@ -267,18 +274,19 @@ def tile_bonsailayer_pa_kernel(tc, X, Z, W, V, th, out):
                 )
 
         def multiply(g, name, s, accs):
-            cols = groups[g][1] * CLASSES
             codes, scales = code_tiles[(g, name)]
             acc = psum_products.tile([P, GROUP_NODES * CLASSES], F32, name=name + "x", tag=name + "x", bufs=BUFS[name])
-            nc.tensor.matmul_mx(
-                out=acc[:, :cols],
-                lhsT=xq_codes[:, s * P : (s + 1) * P].bitcast(FP8X4),
-                lhsT_scale=xq_scales[:, s * P : (s + 1) * P],
-                rhs=codes[:, :cols].bitcast(FP8X4),
-                rhs_scale=scales[:, :cols],
-                start=True,
-                stop=True,
-            )
+            for first, size in node_runs(groups[g][1]):
+                cols = slice(first * CLASSES, (first + size) * CLASSES)
+                nc.tensor.matmul_mx(
+                    out=acc[:, cols],
+                    lhsT=xq_codes[:, s * P : (s + 1) * P].bitcast(FP8X4),
+                    lhsT_scale=xq_scales[:, s * P : (s + 1) * P],
+                    rhs=codes[:, cols].bitcast(FP8X4),
+                    rhs_scale=scales[:, cols],
+                    start=True,
+                    stop=True,
+                )
             accs[(name, s)] = acc
 
         def combine(g, s, accs):
@@ -379,7 +387,7 @@ def tile_bonsailayer_pa_kernel(tc, X, Z, W, V, th, out):
                     transpose_matrix(g + 2, name, COPIES_V if h == 0 else COPIES_W)
                 if not SUMS_FIRST and earlier is not None:
                     add_step(*earlier)
-                if g == DIRECT_FROM and h == 0:
+                if g == DIRECT_FROM and h == SUMS_AT:
                     for s in POOL_TILES + VEC_TILES:
                         add_to_score(s, sums[s], GROUP_NODES, opens=not score_opened)
                         score_opened.append(s)

@@ -41,6 +41,15 @@ SUMS_AT = 1
 
 BUFS = {"words": 3, "v": 2, "w": 2}
 MX_ORDER = (("v", 0), ("w", 0), ("v", 1), ("w", 1), ("v", 2), ("w", 2), ("v", 3), ("w", 3))
+STEP = 2
+VCOPY = 999
+SUMMED = {0: 4, 1: 0, 2: 4, 3: 0}
+SUMS_TILE = 62
+ORDER_AHEAD = 2
+ORDER_EVERY = 2
+FIN = 0
+S_BANK = 2
+ORDERS = {1: "v0 w0 c0", 2: "v0 v1 w0 w1 c0 c1", 3: "v0 v1 w0 w1 c0 w2 v2 c1 c2", 4: "v0 v1 w0 w1 c0 w2 v2 c1 v3 w3 c2 c3"}
 QW_AFTER = 1
 RE_AFTER = 2
 REORDER = ()
@@ -49,7 +58,7 @@ COPIES_VI = SS
 COPIES_WI = SS
 PRODUCT_BUFS = 8
 POOL_TILES = ()
-DIRECT_FROM = 15
+DIRECT_FROM = 13
 
 FLOPS = 2 * PROJECTED * SAMPLES * FEATURES + 2 * 2 * NODES * CLASSES * SAMPLES * PROJECTED
 
@@ -130,12 +139,15 @@ def tile_bonsailayer_pa_kernel(tc, X, Z, W, V, th, out):
             for name in MATRICES:
                 load_matrix(g, name)
 
-        def transpose_blocks(words, blocks, grouped_words, copy):
+        def transpose_blocks(words, blocks, grouped_words, copy, ordered={}):
             bank = psum_words.tile([P, BANK_BLOCKS, HALVES, P], F32, name="bank", tag="bank")
             for a in range(blocks):
                 for u in range(HALVES):
                     first_word = a * HALVES * P
-                    part = words[:, first_word + u : first_word + HALVES * P : HALVES]
+                    if a in ordered:
+                        part = ordered[a][:, u, :]
+                    else:
+                        part = words[:, first_word + u : first_word + HALVES * P : HALVES]
                     nc.tensor.transpose(bank[:, a, u, :], part, ident_f32[:])
             copy(
                 out=grouped_words.rearrange("q (a r u) -> q a r u", a=blocks, u=HALVES),
@@ -237,17 +249,33 @@ def tile_bonsailayer_pa_kernel(tc, X, Z, W, V, th, out):
         score = psum_score.tile([P, SAMPLES], F32, name="score")
         sums = {s: consts.tile([P, GROUP_NODES * CLASSES], F32, name="sum_%d" % s) for s in POOL_TILES + VEC_TILES}
 
-        def transpose_matrix(g, name, copies):
+        def transpose_bank(g, name, bank_of_matrix, copy):
             count = groups[g][1]
             block_words = PROJECTED // 2
             words = raw_tiles[(g, name)][:].bitcast(F32)
-            grouped = grouped_pool.tile([P, GROUP_NODES * PROJECTED], BF16, name="grouped_" + name, tag="grouped_" + name, align_bytes=64)
-            grouped_words = grouped[:].bitcast(F32)
-            for j in range(0, count, BANK_BLOCKS):
-                blocks = min(BANK_BLOCKS, count - j)
-                part = slice(j * block_words, (j + blocks) * block_words)
-                transpose_blocks(words[:, part], blocks, grouped_words[:, part], copies[j // BANK_BLOCKS])
-            grouped_tiles[(g, name)] = grouped
+            if bank_of_matrix == 0:
+                grouped_tiles[(g, name)] = grouped_pool.tile([P, GROUP_NODES * PROJECTED], BF16, name="grouped_" + name, tag="grouped_" + name, align_bytes=64)
+            grouped_words = grouped_tiles[(g, name)][:].bitcast(F32)
+            j = bank_of_matrix * BANK_BLOCKS
+            blocks = min(BANK_BLOCKS, count - j)
+            part = slice(j * block_words, (j + blocks) * block_words)
+            transpose_blocks(words[:, part], blocks, grouped_words[:, part], copy, ordered_blocks.get((g, name, bank_of_matrix), {}))
+
+        ordered_blocks = {}
+
+        def order_block(g, name, bank_of_matrix, a, copy):
+            count = groups[g][1]
+            j = bank_of_matrix * BANK_BLOCKS + a
+            if j >= count:
+                return
+            words = raw_tiles[(g, name)][:].bitcast(F32)[:, j * HALVES * P : (j + 1) * HALVES * P]
+            ordered = work.tile([P, HALVES, P], F32, name="ordered", tag="ordered")
+            copy(out=ordered[:], in_=words.rearrange("c (q u) -> c u q", u=HALVES))
+            ordered_blocks.setdefault((g, name, bank_of_matrix), {})[a] = ordered
+
+        def transpose_matrix(g, name, copies):
+            for bank_of_matrix, copy in enumerate(copies):
+                transpose_bank(g, name, bank_of_matrix, copy)
 
         def quantise_matrix(g, name):
             count = groups[g][1]
@@ -358,43 +386,84 @@ def tile_bonsailayer_pa_kernel(tc, X, Z, W, V, th, out):
         quantise_row_tile("x", 2)
         quantise_row_tile("x", 3)
 
-        earlier = None
         n_groups = len(groups)
-        for g in range(n_groups):
-            for h in range(STEPS):
-                name = MATRICES[h]
-                if g == 0 and h == 1:
-                    project(2)
-                    project(3)
-                    transpose_matrix(1, "w", (by_scalar, by_vector))
-                    quantise_projection(2)
-                    quantise_projection(3)
-                accs = {}
-                s0, s1 = 2 * h, 2 * h + 1
-                if Q_AT == 0 and g + 1 < n_groups:
-                    quantise_matrix(g + 1, name)
-                for m, s in (("v", s0), ("v", s1), ("w", s0), ("w", s1)) if VVWW else (("v", s0), ("w", s0), ("v", s1), ("w", s1)):
-                    multiply(g, m, s, accs)
-                products = [(s0, combine(g, s0, accs))]
-                if Q_AT == 1 and g + 1 < n_groups:
-                    quantise_matrix(g + 1, name)
-                products.append((s1, combine(g, s1, accs)))
-                if Q_AT == 2 and g + 1 < n_groups:
-                    quantise_matrix(g + 1, name)
-                if SUMS_FIRST and earlier is not None:
-                    add_step(*earlier)
-                if g + 2 < n_groups:
-                    transpose_matrix(g + 2, name, COPIES_V if h == 0 else COPIES_W)
-                if not SUMS_FIRST and earlier is not None:
-                    add_step(*earlier)
-                if g == DIRECT_FROM and h == SUMS_AT:
-                    for s in POOL_TILES + VEC_TILES:
-                        add_to_score(s, sums[s], GROUP_NODES, opens=not score_opened)
-                        score_opened.append(s)
-                if g + LOADED_AHEAD < n_groups:
-                    load_matrix(g + LOADED_AHEAD, name)
-                earlier = (g, products)
-        add_step(*earlier)
+        tiles = [(g, s) for g in range(n_groups) for s in range(SAMPLE_TILES)]
+        matrices = [(g, name) for g in range(n_groups) for name in MATRICES]
+        pending = []
+
+        def add_pending(most):
+            for i in range(min(most, len(pending))):
+                s, products, j = pending.pop(0)
+                add_to_score(s, products[:, j * CLASSES : (j + 1) * CLASSES], 1, opens=not score_opened)
+                score_opened.append(s)
+
+        def finish(done):
+            for g, s, products in done:
+                count = groups[g][1]
+                summed = SUMMED[s] if g < DIRECT_FROM else 0
+                if summed and g > 0:
+                    engine = nc.vector if s in VEC_TILES else nc.gpsimd
+                    cs = slice(0, summed * CLASSES)
+                    engine.tensor_tensor(out=sums[s][:, cs], in0=sums[s][:, cs], in1=products[:, cs], op=ADD)
+                pending.extend([(s, products, j) for j in range(summed, count)])
+
+        done = []
+        first = 0
+        while first < len(tiles):
+            size = STEP if first >= SAMPLE_TILES else 2
+            step = range(first, min(first + size, len(tiles)))
+            if first == 2:
+                project(2)
+                project(3)
+                quantise_projection(2)
+                quantise_projection(3)
+                transpose_matrix(1, "w", (by_scalar, by_vector))
+            accs = {}
+            now = []
+            def due(i):
+                if i % 2 == 0 and i // 2 + 2 < len(matrices):
+                    quantise_matrix(*matrices[i // 2 + 2])
+            if Q_AT == 0:
+                for i in step:
+                    due(i)
+            for token in ORDERS[len(step)].split(" "):
+                i = first + int(token[1])
+                g, s = tiles[i]
+                if token[0] == "c":
+                    if Q_AT == 1:
+                        due(i)
+                    now.append((g, s, combine(g, s, accs)))
+                else:
+                    multiply(g, token[0], s, accs)
+            for i in step:
+                n = i + 2 * SAMPLE_TILES + ORDER_AHEAD
+                if n < len(tiles) and n % ORDER_EVERY == ORDER_EVERY - 1:
+                    g, name = matrices[n // 2]
+                    order_block(g, name, n % 2, 0, by_scalar)
+            if FIN == 0:
+                finish(done)
+            for i in step:
+                n = i + 2 * SAMPLE_TILES
+                if n < len(tiles):
+                    g, name = matrices[n // 2]
+                    transpose_bank(g, name, n % 2, by_vector if n % VCOPY == VCOPY - 1 else by_scalar)
+                    add_pending(S_BANK)
+                    if n % 2 == 1 and n // 2 - 4 + 2 * LOADED_AHEAD < len(matrices):
+                        load_matrix(*matrices[n // 2 - 4 + 2 * LOADED_AHEAD])
+            if first == SUMS_TILE:
+                for s in POOL_TILES + VEC_TILES:
+                    pending.extend([(s, sums[s], j) for j in range(SUMMED[s])])
+            add_pending(len(pending) if FIN == 0 else 0)
+            if FIN == 1:
+                finish(done)
+                add_pending(len(pending))
+            done = now
+            first += len(step)
+        finish(done)
+        while len(pending) > 1:
+            add_pending(1)
+        s, products, j = pending.pop(0)
+        add_to_score(s, products[:, j * CLASSES : (j + 1) * CLASSES], 1, closes=True)
 
         result = consts.tile([P, SAMPLES], F32, name="result")
         nc.scalar.copy(out=result[:], in_=score[:])

@@ -32,7 +32,7 @@ MATRICES = ("v", "w")
 LOADED_AHEAD = 6
 RAW_BUFS = 8
 ADD_PARTS = 2
-VEC_TILES = (0, 2)
+VEC_TILES = (0, 3)
 Q_AT = 0
 VVWW = True
 SUMS_FIRST = False
@@ -43,10 +43,8 @@ BUFS = {"words": 3, "v": 2, "w": 2}
 MX_ORDER = (("v", 0), ("w", 0), ("v", 1), ("w", 1), ("v", 2), ("w", 2), ("v", 3), ("w", 3))
 STEP = 2
 VCOPY = 999
-SUMMED = {0: 4, 1: 0, 2: 4, 3: 0}
+SUMMED = {0: 4, 1: 4, 2: 0, 3: 4}
 SUMS_TILE = 62
-ORDER_AHEAD = 2
-ORDER_EVERY = 2
 FIN = 0
 S_BANK = 2
 ORDERS = {1: "v0 w0 c0", 2: "v0 v1 w0 w1 c0 c1", 3: "v0 v1 w0 w1 c0 w2 v2 c1 c2", 4: "v0 v1 w0 w1 c0 w2 v2 c1 v3 w3 c2 c3"}
@@ -57,7 +55,7 @@ SS, SV, VS = (0, 0), (0, 1), (1, 0)
 COPIES_VI = SS
 COPIES_WI = SS
 PRODUCT_BUFS = 8
-POOL_TILES = ()
+POOL_TILES = (1,)
 DIRECT_FROM = 13
 
 FLOPS = 2 * PROJECTED * SAMPLES * FEATURES + 2 * 2 * NODES * CLASSES * SAMPLES * PROJECTED
@@ -139,15 +137,12 @@ def tile_bonsailayer_pa_kernel(tc, X, Z, W, V, th, out):
             for name in MATRICES:
                 load_matrix(g, name)
 
-        def transpose_blocks(words, blocks, grouped_words, copy, ordered={}):
+        def transpose_blocks(words, blocks, grouped_words, copy):
             bank = psum_words.tile([P, BANK_BLOCKS, HALVES, P], F32, name="bank", tag="bank")
             for a in range(blocks):
                 for u in range(HALVES):
                     first_word = a * HALVES * P
-                    if a in ordered:
-                        part = ordered[a][:, u, :]
-                    else:
-                        part = words[:, first_word + u : first_word + HALVES * P : HALVES]
+                    part = words[:, first_word + u : first_word + HALVES * P : HALVES]
                     nc.tensor.transpose(bank[:, a, u, :], part, ident_f32[:])
             copy(
                 out=grouped_words.rearrange("q (a r u) -> q a r u", a=blocks, u=HALVES),
@@ -259,19 +254,7 @@ def tile_bonsailayer_pa_kernel(tc, X, Z, W, V, th, out):
             j = bank_of_matrix * BANK_BLOCKS
             blocks = min(BANK_BLOCKS, count - j)
             part = slice(j * block_words, (j + blocks) * block_words)
-            transpose_blocks(words[:, part], blocks, grouped_words[:, part], copy, ordered_blocks.get((g, name, bank_of_matrix), {}))
-
-        ordered_blocks = {}
-
-        def order_block(g, name, bank_of_matrix, a, copy):
-            count = groups[g][1]
-            j = bank_of_matrix * BANK_BLOCKS + a
-            if j >= count:
-                return
-            words = raw_tiles[(g, name)][:].bitcast(F32)[:, j * HALVES * P : (j + 1) * HALVES * P]
-            ordered = work.tile([P, HALVES, P], F32, name="ordered", tag="ordered")
-            copy(out=ordered[:], in_=words.rearrange("c (q u) -> c u q", u=HALVES))
-            ordered_blocks.setdefault((g, name, bank_of_matrix), {})[a] = ordered
+            transpose_blocks(words[:, part], blocks, grouped_words[:, part], copy)
 
         def transpose_matrix(g, name, copies):
             for bank_of_matrix, copy in enumerate(copies):
@@ -435,11 +418,6 @@ def tile_bonsailayer_pa_kernel(tc, X, Z, W, V, th, out):
                     now.append((g, s, combine(g, s, accs)))
                 else:
                     multiply(g, token[0], s, accs)
-            for i in step:
-                n = i + 2 * SAMPLE_TILES + ORDER_AHEAD
-                if n < len(tiles) and n % ORDER_EVERY == ORDER_EVERY - 1:
-                    g, name = matrices[n // 2]
-                    order_block(g, name, n % 2, 0, by_scalar)
             if FIN == 0:
                 finish(done)
             for i in step:

@@ -32,7 +32,7 @@ MATRICES = ("v", "w")
 LOADED_AHEAD = 6
 RAW_BUFS = 8
 ADD_PARTS = 2
-VEC_TILES = (0, 3)
+VEC_TILES = (0,)
 Q_AT = 0
 VVWW = True
 SUMS_FIRST = False
@@ -55,7 +55,7 @@ SS, SV, VS = (0, 0), (0, 1), (1, 0)
 COPIES_VI = SS
 COPIES_WI = SS
 PRODUCT_BUFS = 8
-POOL_TILES = (1,)
+POOL_TILES = (1, 3)
 DIRECT_FROM = 13
 
 FLOPS = 2 * PROJECTED * SAMPLES * FEATURES + 2 * 2 * NODES * CLASSES * SAMPLES * PROJECTED

@@ -42,11 +42,13 @@ SUMS_AT = 1
 BUFS = {"words": 3, "v": 2, "w": 2}
 MX_ORDER = (("v", 0), ("w", 0), ("v", 1), ("w", 1), ("v", 2), ("w", 2), ("v", 3), ("w", 3))
 STEP = 2
+CUT = True
+LAST_SUMMED = {0: 13, 1: 15, 3: 15}
 VCOPY = 999
-SUMMED = {0: 4, 1: 4, 2: 0, 3: 4}
+SUMMED = {0: 3, 1: 4, 2: 0, 3: 4}
 SUMS_TILE = 62
 FIN = 0
-S_BANK = 2
+S_BANK = 0
 ORDERS = {1: "v0 w0 c0", 2: "v0 v1 w0 w1 c0 c1", 3: "v0 v1 w0 w1 c0 w2 v2 c1 c2", 4: "v0 v1 w0 w1 c0 w2 v2 c1 v3 w3 c2 c3"}
 QW_AFTER = 1
 RE_AFTER = 2
@@ -353,9 +355,9 @@ def tile_bonsailayer_pa_kernel(tc, X, Z, W, V, th, out):
         transpose_row_tile("x", 1, by_scalar)
         quantise_row_tile("z", 3)
         quantise_row_tile("x", 0)
-        path_probabilities()
         quantise_row_tile("x", 1)
         transpose_matrix(0, "v", (by_scalar, by_vector))
+        path_probabilities()
         project(0)
         project(1)
         quantise_matrix(0, "v")
@@ -374,16 +376,17 @@ def tile_bonsailayer_pa_kernel(tc, X, Z, W, V, th, out):
         matrices = [(g, name) for g in range(n_groups) for name in MATRICES]
         pending = []
 
-        def add_pending(most):
-            for i in range(min(most, len(pending))):
+        def add_pending(most, closes=False):
+            count = min(most, len(pending))
+            for i in range(count):
                 s, products, j = pending.pop(0)
-                add_to_score(s, products[:, j * CLASSES : (j + 1) * CLASSES], 1, opens=not score_opened)
+                add_to_score(s, products[:, j * CLASSES : (j + 1) * CLASSES], 1, opens=not score_opened, closes=closes and i == count - 1)
                 score_opened.append(s)
 
         def finish(done):
             for g, s, products in done:
                 count = groups[g][1]
-                summed = SUMMED[s] if g < DIRECT_FROM else 0
+                summed = SUMMED[s] if g < LAST_SUMMED.get(s, 0) else 0
                 if summed and g > 0:
                     engine = nc.vector if s in VEC_TILES else nc.gpsimd
                     cs = slice(0, summed * CLASSES)
@@ -431,18 +434,29 @@ def tile_bonsailayer_pa_kernel(tc, X, Z, W, V, th, out):
             if first == SUMS_TILE:
                 for s in POOL_TILES + VEC_TILES:
                     pending.extend([(s, sums[s], j) for j in range(SUMMED[s])])
-            add_pending(len(pending) if FIN == 0 else 0)
-            if FIN == 1:
-                finish(done)
-                add_pending(len(pending))
+            add_pending(len(pending), closes=CUT and first == len(tiles) - 2)
             done = now
             first += len(step)
         finish(done)
-        while len(pending) > 1:
-            add_pending(1)
-        s, products, j = pending.pop(0)
-        add_to_score(s, products[:, j * CLASSES : (j + 1) * CLASSES], 1, closes=True)
-
         result = consts.tile([P, SAMPLES], F32, name="result")
-        nc.scalar.copy(out=result[:], in_=score[:])
-        nc.sync.dma_start(out=out, in_=result[:])
+        early = consts.tile([P, SAMPLES // 2], F32, name="early")
+        if CUT:
+            nc.scalar.copy(out=early[:], in_=score[:, SAMPLES // 2 :])
+            nc.scalar.copy(out=result[:, : SAMPLES // 2], in_=score[:, : SAMPLES // 2])
+            nc.sync.dma_start(out=out[:, : SAMPLES // 2], in_=result[:, : SAMPLES // 2])
+            last = psum_words.tile([P, SAMPLES // 2], F32, name="last", tag="bank")
+            for i, (s, products, j) in enumerate(pending):
+                nc.tensor.matmul(
+                    out=last[:, (s - 2) * P : (s - 1) * P],
+                    lhsT=products[:, j * CLASSES : (j + 1) * CLASSES],
+                    rhs=ident_f32[:],
+                    is_transpose=True,
+                    start=(i == 0),
+                    stop=(i == len(pending) - 1),
+                )
+            nc.vector.tensor_tensor(out=result[:, SAMPLES // 2 :], in0=last[:], in1=early[:], op=ADD)
+            nc.sync.dma_start(out=out[:, SAMPLES // 2 :], in_=result[:, SAMPLES // 2 :])
+        else:
+            add_pending(len(pending), closes=True)
+            nc.scalar.copy(out=result[:], in_=score[:])
+            nc.sync.dma_start(out=out, in_=result[:])

from contextlib import ExitStack

import concourse.mybir as mybir
from concourse.masks import make_identity

F32 = mybir.dt.float32
BF16 = mybir.dt.bfloat16
U32 = mybir.dt.uint32
U8 = mybir.dt.uint8
FP8X4 = mybir.dt.float8_e4m3fn_x4
ADD = mybir.AluOpType.add
MULT = mybir.AluOpType.mult
TANH = mybir.ActivationFunctionType.Tanh

P = 128
PACK = 4
K_PASS = P * PACK
HALVES = 2

SAMPLES, FEATURES, PROJECTED, CLASSES = 512, 1024, 512, 128
DEPTH = 5
INNER_NODES = (1 << DEPTH) - 1
NODES = 2 * INNER_NODES + 1
SAMPLE_TILES = SAMPLES // P
FEATURE_PASSES = FEATURES // K_PASS
GROUP_NODES = 4
BANK_BLOCKS = 2

STEP_TILES = 2
STEPS = SAMPLE_TILES // STEP_TILES
MATRICES = ("v", "w")
LOADED_AHEAD = 6
RAW_BUFS = 8
ADD_PARTS = 2
VEC_TILES = (0,)
Q_AT = 0
VVWW = True
SUMS_FIRST = False
SUMS_AT = 1


BUFS = {"words": 3, "v": 2, "w": 2}
MX_ORDER = (("v", 0), ("w", 0), ("v", 1), ("w", 1), ("v", 2), ("w", 2), ("v", 3), ("w", 3))
STEP = 2
CUT = True
LAST_SUMMED = {0: 13, 1: 15, 3: 15}
VCOPY = 999
SUMMED = {0: 3, 1: 4, 2: 0, 3: 4}
SUMS_TILE = 62
FIN = 0
S_BANK = 0
ORDERS = {1: "v0 w0 c0", 2: "v0 v1 w0 w1 c0 c1", 3: "v0 v1 w0 w1 c0 w2 v2 c1 c2", 4: "v0 v1 w0 w1 c0 w2 v2 c1 v3 w3 c2 c3"}
QW_AFTER = 1
RE_AFTER = 2
REORDER = ()
SS, SV, VS = (0, 0), (0, 1), (1, 0)
COPIES_VI = SS
COPIES_WI = SS
PRODUCT_BUFS = 8
POOL_TILES = (1, 3)
DIRECT_FROM = 13

FLOPS = 2 * PROJECTED * SAMPLES * FEATURES + 2 * 2 * NODES * CLASSES * SAMPLES * PROJECTED


def node_groups():
    return [(first, min(GROUP_NODES, NODES - first)) for first in range(0, NODES, GROUP_NODES)]


def node_runs(count):
    runs = []
    first = 0
    for size in (4, 2, 1):
        while count - first >= size:
            runs.append((first, size))
            first += size
    return runs


def tile_bonsailayer_pa_kernel(tc, X, Z, W, V, th, out):
    nc = tc.nc
    groups = node_groups()

    with ExitStack() as ctx:
        consts = ctx.enter_context(tc.tile_pool(name="consts", bufs=1))
        first_stage = ctx.enter_context(tc.tile_pool(name="first_stage", bufs=4))
        raw_pool = ctx.enter_context(tc.tile_pool(name="raw", bufs=RAW_BUFS))
        grouped_pool = ctx.enter_context(tc.tile_pool(name="grouped", bufs=3))
        codes_pool = ctx.enter_context(tc.tile_pool(name="codes", bufs=3))
        work = ctx.enter_context(tc.tile_pool(name="work", bufs=4))
        psum_words = ctx.enter_context(tc.psum_pool(name="psum_words", bufs=BUFS["words"]))
        psum_products = ctx.enter_context(tc.psum_pool(name="psum_products", bufs=2))
        psum_score = ctx.enter_context(tc.psum_pool(name="psum_score", bufs=1))
        ctx.enter_context(tc.manual_schedule())

        ident_f32 = consts.tile([P, P], F32, name="ident_f32")
        make_identity(nc, ident_f32[:])
        ident_bf16 = consts.tile([P, P], BF16, name="ident_bf16")
        make_identity(nc, ident_bf16[:])

        th_rows = consts.tile([P, SAMPLES], BF16, name="th_rows")
        nc.vector.memset(th_rows[:], 0.0)
        nc.scalar.dma_start(out=th_rows[:INNER_NODES, :], in_=th)

        warm = consts.tile([P, 1], F32, name="warm")
        nc.vector.memset(warm[:], 0.0)
        nc.scalar.activation(out=warm[:], in_=warm[:], func=TANH)

        z_raw = consts.tile([P, PACK * FEATURES], BF16, name="z_raw")
        x_raw = consts.tile([P, SAMPLE_TILES * FEATURES], BF16, name="x_raw")
        raw_tiles = {}

        def load_z(t):
            cols = slice(t * FEATURES, (t + 1) * FEATURES)
            nc.sync.dma_start(out=z_raw[:, cols], in_=Z.rearrange("(q t) d -> q (t d)", t=PACK)[:, cols])

        def load_x(s):
            nc.sync.dma_start(out=x_raw[:, s * FEATURES : (s + 1) * FEATURES], in_=X[s * P : (s + 1) * P, :])

        def load_matrix(g, name):
            first_node, count = groups[g]
            matrix = V if name == "v" else W
            raw = raw_pool.tile([P, GROUP_NODES * PROJECTED], BF16, name="raw_" + name, tag="raw_" + name)
            nc.sync.dma_start(
                out=raw[:, : count * PROJECTED].rearrange("c (j k) -> c j k", j=count),
                in_=matrix[first_node * P : (first_node + count) * P, :].rearrange("(j c) k -> c j k", c=P),
            )
            raw_tiles[(g, name)] = raw

        for t in range(PACK):
            load_z(t)
        load_x(0)
        load_x(1)
        load_matrix(0, "v")
        load_matrix(0, "w")
        load_x(2)
        load_x(3)
        for g in range(1, LOADED_AHEAD):
            for name in MATRICES:
                load_matrix(g, name)

        def transpose_blocks(words, blocks, grouped_words, copy):
            bank = psum_words.tile([P, BANK_BLOCKS, HALVES, P], F32, name="bank", tag="bank")
            for a in range(blocks):
                for u in range(HALVES):
                    first_word = a * HALVES * P
                    part = words[:, first_word + u : first_word + HALVES * P : HALVES]
                    nc.tensor.transpose(bank[:, a, u, :], part, ident_f32[:])
            copy(
                out=grouped_words.rearrange("q (a r u) -> q a r u", a=blocks, u=HALVES),
                in_=bank[:, :blocks].rearrange("q a u r -> q a r u"),
            )

        def quantise(grouped, codes, scales):
            nc.vector.quantize_mx(out=codes.bitcast(FP8X4), scales=scales, in_=grouped)

        z_codes = consts.tile([P, PACK * FEATURE_PASSES * P], U32, name="z_codes", align_bytes=64)
        z_scales = consts.tile([P, PACK * FEATURE_PASSES * P], U8, name="z_scales", align_bytes=64)
        x_codes = consts.tile([P, SAMPLE_TILES * FEATURE_PASSES * P], U32, name="x_codes", align_bytes=64)
        x_scales = consts.tile([P, SAMPLE_TILES * FEATURE_PASSES * P], U8, name="x_scales", align_bytes=64)
        first_stage_operands = {"z": (z_raw, z_codes, z_scales), "x": (x_raw, x_codes, x_scales)}
        first_stage_grouped = {}

        def transpose_row_tile(name, r, copy):
            raw = first_stage_operands[name][0]
            words = raw[:].bitcast(F32)
            row_words = FEATURES // 2
            grouped = first_stage.tile([P, FEATURES], BF16, name="row_grouped", tag="row_grouped", align_bytes=64)
            transpose_blocks(
                words[:, r * row_words : (r + 1) * row_words], FEATURE_PASSES, grouped[:].bitcast(F32), copy
            )
            first_stage_grouped[(name, r)] = grouped

        def quantise_row_tile(name, r):
            codes, scales = first_stage_operands[name][1:]
            cols = FEATURE_PASSES * P
            quantise(
                first_stage_grouped[(name, r)][:],
                codes[:, r * cols : (r + 1) * cols],
                scales[:, r * cols : (r + 1) * cols],
            )

        xq_codes = consts.tile([P, SAMPLES], U32, name="xq_codes", align_bytes=64)
        xq_scales = consts.tile([P, SAMPLES], U8, name="xq_scales", align_bytes=64)
        xp_grouped_tiles = {}

        def project(s):
            xp = psum_products.tile([P, PACK, P], F32, name="xp", tag="wx", bufs=BUFS["w"])
            for t in range(PACK):
                for g in range(FEATURE_PASSES):
                    z_cols = slice((t * FEATURE_PASSES + g) * P, (t * FEATURE_PASSES + g + 1) * P)
                    x_cols = slice((s * FEATURE_PASSES + g) * P, (s * FEATURE_PASSES + g + 1) * P)
                    nc.tensor.matmul_mx(
                        out=xp[:, t, :],
                        lhsT=z_codes[:, z_cols].bitcast(FP8X4),
                        lhsT_scale=z_scales[:, z_cols],
                        rhs=x_codes[:, x_cols].bitcast(FP8X4),
                        rhs_scale=x_scales[:, x_cols],
                        start=(g == 0),
                        stop=(g == FEATURE_PASSES - 1),
                    )
            xp_grouped = first_stage.tile([P, P * PACK], BF16, name="xp_grouped", tag="xp_grouped", align_bytes=64)
            nc.scalar.mul(
                out=xp_grouped[:].rearrange("q (b t) -> q b t", t=PACK),
                in_=xp[:].rearrange("q t b -> q b t"),
                mul=1.0 / PROJECTED,
            )
            xp_grouped_tiles[s] = xp_grouped

        def quantise_projection(s):
            quantise(xp_grouped_tiles[s][:], xq_codes[:, s * P : (s + 1) * P], xq_scales[:, s * P : (s + 1) * P])

        prob = consts.tile([P, SAMPLE_TILES, NODES], F32, name="prob")

        def path_probabilities():
            th_cols = psum_words.tile([P, SAMPLE_TILES, P], BF16, name="th_cols", tag="bank")
            for s in range(SAMPLE_TILES):
                nc.tensor.transpose(th_cols[:, s, :], th_rows[:, s * P : (s + 1) * P], ident_bf16[:])
            branch = consts.tile([P, SAMPLE_TILES, INNER_NODES, 2], F32, name="branch")
            for side, sign in ((0, 0.5), (1, -0.5)):
                nc.vector.tensor_scalar(
                    out=branch[:, :, :, side],
                    in0=th_cols[:, :, :INNER_NODES],
                    scalar1=sign,
                    scalar2=0.5,
                    op0=MULT,
                    op1=ADD,
                )
            nc.gpsimd.memset(prob[:, :, 0:1], 1.0)
            first = 0
            for depth in range(DEPTH):
                width = 1 << depth
                child = 2 * first + 1
                nc.gpsimd.tensor_tensor(
                    out=prob[:, :, child : child + 2 * width].rearrange("b s (i c) -> b s i c", c=2),
                    in0=branch[:, :, first : first + width, :],
                    in1=prob[:, :, first : first + width]
                    .unsqueeze(3)
                    .to_broadcast([P, SAMPLE_TILES, width, 2]),
                    op=MULT,
                )
                first = child

        grouped_tiles = {}
        code_tiles = {}
        score = psum_score.tile([P, SAMPLES], F32, name="score")
        sums = {s: consts.tile([P, GROUP_NODES * CLASSES], F32, name="sum_%d" % s) for s in POOL_TILES + VEC_TILES}

        def transpose_bank(g, name, bank_of_matrix, copy):
            count = groups[g][1]
            block_words = PROJECTED // 2
            words = raw_tiles[(g, name)][:].bitcast(F32)
            if bank_of_matrix == 0:
                grouped_tiles[(g, name)] = grouped_pool.tile([P, GROUP_NODES * PROJECTED], BF16, name="grouped_" + name, tag="grouped_" + name, align_bytes=64)
            grouped_words = grouped_tiles[(g, name)][:].bitcast(F32)
            j = bank_of_matrix * BANK_BLOCKS
            blocks = min(BANK_BLOCKS, count - j)
            part = slice(j * block_words, (j + blocks) * block_words)
            transpose_blocks(words[:, part], blocks, grouped_words[:, part], copy)

        def transpose_matrix(g, name, copies):
            for bank_of_matrix, copy in enumerate(copies):
                transpose_bank(g, name, bank_of_matrix, copy)

        def quantise_matrix(g, name):
            count = groups[g][1]
            codes = codes_pool.tile([P, GROUP_NODES * CLASSES], U32, name="codes_" + name, tag="codes_" + name, align_bytes=64)
            scales = codes_pool.tile([P, GROUP_NODES * CLASSES], U8, name="scales_" + name, tag="scales_" + name, align_bytes=64)
            for first, size in node_runs(count):
                cols = slice(first * CLASSES, (first + size) * CLASSES)
                quantise(
                    grouped_tiles[(g, name)][:, first * PROJECTED : (first + size) * PROJECTED],
                    codes[:, cols],
                    scales[:, cols],
                )
            code_tiles[(g, name)] = (codes, scales)

        def add_to_score(s, products, count, opens=False, closes=False):
            for j in range(count):
                nc.tensor.matmul(
                    out=score[:, s * P : (s + 1) * P],
                    lhsT=products[:, j * CLASSES : (j + 1) * CLASSES],
                    rhs=ident_f32[:],
                    is_transpose=True,
                    start=(opens and j == 0),
                    stop=(closes and j == count - 1),
                )

        def multiply(g, name, s, accs):
            codes, scales = code_tiles[(g, name)]
            acc = psum_products.tile([P, GROUP_NODES * CLASSES], F32, name=name + "x", tag=name + "x", bufs=BUFS[name])
            for first, size in node_runs(groups[g][1]):
                cols = slice(first * CLASSES, (first + size) * CLASSES)
                nc.tensor.matmul_mx(
                    out=acc[:, cols],
                    lhsT=xq_codes[:, s * P : (s + 1) * P].bitcast(FP8X4),
                    lhsT_scale=xq_scales[:, s * P : (s + 1) * P],
                    rhs=codes[:, cols].bitcast(FP8X4),
                    rhs_scale=scales[:, cols],
                    start=True,
                    stop=True,
                )
            accs[(name, s)] = acc

        def combine(g, s, accs):
            first_node, count = groups[g]
            cols = count * CLASSES
            tanh_vx = work.tile([P, GROUP_NODES * CLASSES], F32, name="tanh_vx", tag="tanh_vx")
            nc.scalar.activation(out=tanh_vx[:, :cols], in_=accs[("v", s)][:, :cols], func=TANH)
            if g == 0 and s in POOL_TILES + VEC_TILES:
                products = sums[s]
            else:
                products = work.tile([P, GROUP_NODES * CLASSES], F32, name="products", tag="products", bufs=PRODUCT_BUFS)
            for j in range(count):
                node_cols = slice(j * CLASSES, (j + 1) * CLASSES)
                nc.vector.scalar_tensor_tensor(
                    out=products[:, node_cols],
                    in0=accs[("w", s)][:, node_cols],
                    scalar=prob[:, s, first_node + j : first_node + j + 1],
                    in1=tanh_vx[:, node_cols],
                    op0=MULT,
                    op1=MULT,
                )
            return products

        score_opened = []

        def add_step(g, step_products):
            count = groups[g][1]
            cols = count * CLASSES
            for s, products in step_products:
                if s in POOL_TILES + VEC_TILES and g < DIRECT_FROM:
                    if g > 0:
                        engine = nc.gpsimd if s in POOL_TILES else nc.vector
                        part = cols // ADD_PARTS if s in POOL_TILES else cols
                        for c in range(0, cols, part):
                            cs = slice(c, c + part)
                            engine.tensor_tensor(out=sums[s][:, cs], in0=sums[s][:, cs], in1=products[:, cs], op=ADD)
                else:
                    last = g == len(groups) - 1 and s == SAMPLE_TILES - 1
                    add_to_score(s, products, count, opens=not score_opened, closes=last)
                    score_opened.append(s)

        by_scalar, by_vector = nc.scalar.copy, nc.vector.tensor_copy
        COPIES_V = [(by_scalar, by_vector)[i] for i in COPIES_VI]
        COPIES_W = [(by_scalar, by_vector)[i] for i in COPIES_WI]
        transpose_row_tile("z", 0, by_scalar)
        transpose_row_tile("z", 1, by_vector)
        transpose_row_tile("z", 2, by_scalar)
        quantise_row_tile("z", 0)
        transpose_row_tile("z", 3, by_scalar)
        quantise_row_tile("z", 1)
        transpose_row_tile("x", 0, by_vector)
        quantise_row_tile("z", 2)
        transpose_row_tile("x", 1, by_scalar)
        quantise_row_tile("z", 3)
        quantise_row_tile("x", 0)
        quantise_row_tile("x", 1)
        transpose_matrix(0, "v", (by_scalar, by_vector))
        path_probabilities()
        project(0)
        project(1)
        quantise_matrix(0, "v")
        transpose_matrix(0, "w", (by_scalar, by_vector))
        quantise_projection(0)
        quantise_projection(1)
        transpose_row_tile("x", 2, by_scalar)
        quantise_matrix(0, "w")
        transpose_row_tile("x", 3, by_scalar)
        transpose_matrix(1, "v", (by_vector, by_scalar))
        quantise_row_tile("x", 2)
        quantise_row_tile("x", 3)

        n_groups = len(groups)
        tiles = [(g, s) for g in range(n_groups) for s in range(SAMPLE_TILES)]
        matrices = [(g, name) for g in range(n_groups) for name in MATRICES]
        pending = []

        def add_pending(most, closes=False):
            count = min(most, len(pending))
            for i in range(count):
                s, products, j = pending.pop(0)
                add_to_score(s, products[:, j * CLASSES : (j + 1) * CLASSES], 1, opens=not score_opened, closes=closes and i == count - 1)
                score_opened.append(s)

        def finish(done):
            for g, s, products in done:
                count = groups[g][1]
                summed = SUMMED[s] if g < LAST_SUMMED.get(s, 0) else 0
                if summed and g > 0:
                    engine = nc.vector if s in VEC_TILES else nc.gpsimd
                    cs = slice(0, summed * CLASSES)
                    engine.tensor_tensor(out=sums[s][:, cs], in0=sums[s][:, cs], in1=products[:, cs], op=ADD)
                pending.extend([(s, products, j) for j in range(summed, count)])

        done = []
        first = 0
        while first < len(tiles):
            size = STEP if first >= SAMPLE_TILES else 2
            step = range(first, min(first + size, len(tiles)))
            if first == 2:
                project(2)
                project(3)
                quantise_projection(2)
                quantise_projection(3)
                transpose_matrix(1, "w", (by_scalar, by_vector))
            accs = {}
            now = []
            def due(i):
                if i % 2 == 0 and i // 2 + 2 < len(matrices):
                    quantise_matrix(*matrices[i // 2 + 2])
            if Q_AT == 0:
                for i in step:
                    due(i)
            for token in ORDERS[len(step)].split(" "):
                i = first + int(token[1])
                g, s = tiles[i]
                if token[0] == "c":
                    if Q_AT == 1:
                        due(i)
                    now.append((g, s, combine(g, s, accs)))
                else:
                    multiply(g, token[0], s, accs)
            if FIN == 0:
                finish(done)
            for i in step:
                n = i + 2 * SAMPLE_TILES
                if n < len(tiles):
                    g, name = matrices[n // 2]
                    transpose_bank(g, name, n % 2, by_vector if n % VCOPY == VCOPY - 1 else by_scalar)
                    add_pending(S_BANK)
                    if n % 2 == 1 and n // 2 - 4 + 2 * LOADED_AHEAD < len(matrices):
                        load_matrix(*matrices[n // 2 - 4 + 2 * LOADED_AHEAD])
            if first == SUMS_TILE:
                for s in POOL_TILES + VEC_TILES:
                    pending.extend([(s, sums[s], j) for j in range(SUMMED[s])])
            add_pending(len(pending), closes=CUT and first == len(tiles) - 2)
            done = now
            first += len(step)
        finish(done)
        result = consts.tile([P, SAMPLES], F32, name="result")
        early = consts.tile([P, SAMPLES // 2], F32, name="early")
        if CUT:
            nc.scalar.copy(out=early[:], in_=score[:, SAMPLES // 2 :])
            nc.scalar.copy(out=result[:, : SAMPLES // 2], in_=score[:, : SAMPLES // 2])
            nc.sync.dma_start(out=out[:, : SAMPLES // 2], in_=result[:, : SAMPLES // 2])
            last = psum_words.tile([P, SAMPLES // 2], F32, name="last", tag="bank")
            for i, (s, products, j) in enumerate(pending):
                nc.tensor.matmul(
                    out=last[:, (s - 2) * P : (s - 1) * P],
                    lhsT=products[:, j * CLASSES : (j + 1) * CLASSES],
                    rhs=ident_f32[:],
                    is_transpose=True,
                    start=(i == 0),
                    stop=(i == len(pending) - 1),
                )
            nc.vector.tensor_tensor(out=result[:, SAMPLES // 2 :], in0=last[:], in1=early[:], op=ADD)
            nc.sync.dma_start(out=out[:, SAMPLES // 2 :], in_=result[:, SAMPLES // 2 :])
        else:
            add_pending(len(pending), closes=True)
            nc.scalar.copy(out=result[:], in_=score[:])
            nc.sync.dma_start(out=out, in_=result[:])
